import numpy as np
import ml_dtypes


def mxq(x, axis, fmt="e4m3"):
    dtype, down = {"e4m3": (ml_dtypes.float8_e4m3fn, 7), "e5m2": (ml_dtypes.float8_e5m2, 14)}[fmt]
    v = np.moveaxis(np.asarray(x, np.float32).astype(ml_dtypes.bfloat16).astype(np.float64), axis, -1)
    blocks = v.reshape(v.shape[:-1] + (-1, 32))
    amax = np.abs(blocks).max(-1, keepdims=True)
    byte = np.maximum(np.where(amax > 0, np.frexp(amax)[1] - 1 + 127, 0) - down, 1)
    scale = np.exp2(byte - 127.0)
    codes = (blocks / scale).astype(np.float32).astype(dtype).astype(np.float64)
    return np.moveaxis((codes * scale).reshape(v.shape), -1, axis)


WIDE = False


def mx_kscale(k):
    if not WIDE:
        return np.ones(k)
    levels = np.array([10, -10, 5, -5, 0])
    if k % 512:
        return np.exp2(np.random.permutation(np.resize(levels, k // 32))).repeat(32)
    a = np.empty((k // 512, 16))
    for p in range(k // 512):
        a[p, :8] = np.random.permutation(np.resize(levels, 8))
        for g in range(8):
            far = levels[np.abs(levels - a[p, g]) >= 10]
            a[p, g + 8] = far[np.random.randint(len(far))]
    return np.exp2(a.ravel()).repeat(32)


BF16 = ml_dtypes.bfloat16


def bf(x):
    return np.asarray(x, np.float32).astype(BF16)


def f64(x):
    return np.asarray(x).astype(np.float64)


E2M1 = np.array([0.0, 0.5, 1.0, 1.5, 2.0, 3.0, 4.0, 6.0, -0.0, -0.5, -1.0, -1.5, -2.0, -3.0, -4.0, -6.0])


def pack_weight(w, fmt):
    k, n = w.shape
    w = f64(bf(w)).reshape(k // 32, 32, n)
    amax = np.abs(w).max(1)
    if fmt == "e4m3":
        byte = np.frexp(amax)[1] - 1 + 127 - 7
    else:
        mant, ex = np.frexp(amax / 6.0)
        byte = np.where(mant > 0.5, ex, ex - 1) + 127
    byte = np.clip(np.where(amax > 0, byte, 1), 1, 254)
    scaled = (w * np.exp2(127.0 - byte)[:, None, :]).reshape(k, n).astype(np.float32)
    by_word = np.ascontiguousarray(scaled.reshape(k // 512, 128, 4, n).transpose(0, 1, 3, 2))
    if fmt == "e4m3":
        words = by_word.astype(ml_dtypes.float8_e4m3fn).view(np.uint8)
    else:
        c = by_word.astype(ml_dtypes.float4_e2m1fn).view(np.uint8) & 0xF
        words = c[..., 0::2] | (c[..., 1::2] << 4)
    return np.ascontiguousarray(words), np.ascontiguousarray(byte.astype(np.uint8).reshape(k // 512, 16, n))


def unpack_weight(words, scales, fmt):
    g, p, n, _ = words.shape
    if fmt == "e4m3":
        vals = np.ascontiguousarray(words).view(ml_dtypes.float8_e4m3fn).astype(np.float64)
    else:
        nib = np.empty((g, p, n, 4), np.uint8)
        nib[..., 0::2] = words & 0xF
        nib[..., 1::2] = words >> 4
        vals = E2M1[nib]
    vals = vals * np.repeat(np.exp2(scales.astype(np.float64) - 127.0), 8, axis=1)[..., None]
    return vals.transpose(0, 1, 3, 2).reshape(g * 512, n)
def pack4(w):
    words, scales = pack_weight(w, "e2m1")
    return words.reshape(words.shape[0], 128, -1), scales


def unpack4(words, scales):
    return unpack_weight(words.reshape(words.shape[0], 128, -1, 2), scales, "e2m1")


B, N, G, L = 8192, 256, 64, 256
N2 = 2 * N
L2 = 2 * L
L_LIMIT = 1.0


def relu(v):
    return np.maximum(v, 0.0)


def draw0():
    s, t = mx_kscale(N2), mx_kscale(L2)
    Volt = bf(np.random.standard_normal((B, N2)) * s)
    IM = np.random.standard_normal((L2, N2)) / np.sqrt(N2) / s[None, :] * t[:, None]
    IM_words, IM_scales = pack4(IM.T)
    Ybr = np.random.standard_normal((L2, L2)) / np.sqrt(L2) / t[None, :]
    Ybr_words, Ybr_scales = pack4(Ybr.T)
    return {
        "Volt": Volt,
        "IM_words": IM_words,
        "IM_scales": IM_scales,
        "Ybr_words": Ybr_words,
        "Ybr_scales": Ybr_scales,
        "n_o_mu_i_u": bf(np.random.standard_normal((B, L))),
    }


def core(Volt, IM_words, IM_scales, Ybr_words, Ybr_scales, n_o_mu_i_u):
    mu = f64(n_o_mu_i_u)
    dv = mxq(f64(Volt), 1, "e4m3") @ unpack4(IM_words, IM_scales)
    Ibr = mxq(dv, 1, "e4m3") @ unpack4(Ybr_words, Ybr_scales)
    i_up = Ibr[:, :L] ** 2 + Ibr[:, L:] ** 2 - L_LIMIT ** 2
    out = np.sum(relu(i_up), axis=1)
    out = out + np.sum(np.abs(mu * i_up), axis=1)
    out = out + np.sum(relu(-mu), axis=1)
    return out


def e4m3fn_bytes(y):
    return np.clip(np.asarray(y, np.float64), -448.0, 448.0).astype(np.float32).astype(ml_dtypes.float8_e4m3fn).view(np.uint8)


def e4m3fn_values(b):
    return np.asarray(b, np.uint8).view(ml_dtypes.float8_e4m3fn).astype(np.float64)


def setup_inputs():
    d = draw0()
    x0 = np.asarray(d['Volt']).astype(np.float64)
    s = (np.max(np.abs(x0), axis=(0,), keepdims=True) / 448.0).astype(np.float32)
    out = {}
    for k, v in d.items():
        if k == 'Volt':
            out['Volt_bytes'] = e4m3fn_bytes(x0 / s.astype(np.float64))
            out['Volt_scale'] = s
        else:
            out[k] = v
    return out


def reference(Volt_bytes, Volt_scale, IM_words, IM_scales, Ybr_words, Ybr_scales, n_o_mu_i_u):
    return core(e4m3fn_values(Volt_bytes) * Volt_scale.astype(np.float64), IM_words, IM_scales, Ybr_words, Ybr_scales, n_o_mu_i_u)

@@ -1,0 +1,294 @@
+from contextlib import ExitStack
+
+import concourse.mybir as mybir
+from concourse.masks import make_identity
+
+F32 = mybir.dt.float32
+BF16 = mybir.dt.bfloat16
+I32 = mybir.dt.int32
+U32 = mybir.dt.uint32
+U8 = mybir.dt.uint8
+FP8 = mybir.dt.float8_e4m3fn
+FP8X4 = mybir.dt.float8_e4m3fn_x4
+FP4X4 = mybir.dt.float4_e2m1fn_x4
+ALU = mybir.AluOpType
+ACT = mybir.ActivationFunctionType
+AX = mybir.AxisListType
+
+B, K, L = 8192, 512, 256
+P = 128
+NT = B // P
+UNIT_SIZES = [2, 2] + [4] * 14 + [2, 2]
+UNITS = [(sum(UNIT_SIZES[:i]), n) for i, n in enumerate(UNIT_SIZES)]
+NU = len(UNITS)
+FLOPS = 2 * 2 * B * K * K
+
+VOLT_CHUNKS = [2, 2, 4, 8, 8, 8, 8, 8, 8, 8]
+MU_TILES = 16
+NQ = NT // MU_TILES
+CAST_UNITS = (0, 1)
+CAST_ON_SCALAR = (1,)
+D_ON_VECTOR = tuple(range(9, NT, 10))
+
+ORDER = (("W", 0), ("T", 0), ("E", 0), ("Q", 0), ("M1", 0), ("A", 0), ("D", 1), ("R", 1), ("M2", 1), ("F", 1), ("G", 2), ("Y", 2), ("B", 2), ("S", 2))
+
+
+def tile_pinnlayer_pa_t_w4_kernel(tc, Volt_bytes, Volt_scale, IM_words, IM_scales, Ybr_words, Ybr_scales, n_o_mu_i_u, out):
+    nc = tc.nc
+    with ExitStack() as ctx:
+        keep = ctx.enter_context(tc.tile_pool(name="keep", bufs=1))
+        flow = ctx.enter_context(tc.tile_pool(name="flow", bufs=4))
+        xt_pool = ctx.enter_context(tc.psum_pool(name="xt_pool", bufs=2))
+        dv_pool = ctx.enter_context(tc.psum_pool(name="dv_pool", bufs=3))
+        ib_pool = ctx.enter_context(tc.psum_pool(name="ib_pool", bufs=3))
+
+        volt_view = Volt_bytes.rearrange("(p j) k -> p j k", p=P)
+        mu_view = n_o_mu_i_u.rearrange("(p j) l -> p j l", p=P)
+
+        im_scales_raw = keep.tile([P, 512], U8, align_bytes=64)
+        yb_scales = keep.tile([P, 512], U8, align_bytes=64)
+        nc.vector.memset(im_scales_raw[:].bitcast(I32), 0)
+        nc.vector.memset(yb_scales[:].bitcast(I32), 0)
+        ident_f32 = keep.tile([P, P], F32)
+        make_identity(nc, ident_f32[:])
+        ident_bf16 = keep.tile([P, P], BF16)
+        make_identity(nc, ident_bf16[:])
+
+        raw_of_tile = {}
+        chunks = []
+        j0 = 0
+        for i, n in enumerate(VOLT_CHUNKS):
+            volt_raw = keep.tile([P, n, K], U8, name="volt_raw_%d" % i)
+            chunks.append((volt_raw, j0, n))
+            for j in range(n):
+                raw_of_tile[j0 + j] = (volt_raw, j)
+            j0 += n
+
+        def load_volt(i):
+            t, first, n = chunks[i]
+            nc.sync.dma_start(out=t[:], in_=volt_view[:, first : first + n, :])
+
+        load_volt(0)
+        scale_cols = keep.tile([P, 4], F32)
+        nc.sync.dma_start(out=scale_cols[:], in_=Volt_scale.rearrange("o (p t) -> p (o t)", t=4))
+        im_words_raw = keep.tile([P, 1024], U8)
+        nc.sync.dma_start(out=im_words_raw[:], in_=IM_words[0])
+        for q in range(4):
+            nc.sync.dma_start(out=im_scales_raw[32 * q : 32 * q + 4, :].bitcast(I32), in_=IM_scales[0, 4 * q : 4 * q + 4, :].bitcast(I32))
+        load_volt(1)
+        scale_rows = keep.tile([P, 4, K], F32)
+        nc.sync.dma_start(out=scale_rows[:, 0, :], in_=Volt_scale.rearrange("o k -> (o k)").partition_broadcast(P))
+        yb_words = keep.tile([P, 1024], U8, align_bytes=64)
+        nc.sync.dma_start(out=yb_words[:], in_=Ybr_words[0])
+        for q in range(4):
+            nc.sync.dma_start(out=yb_scales[32 * q : 32 * q + 4, :].bitcast(I32), in_=Ybr_scales[0, 4 * q : 4 * q + 4, :].bitcast(I32))
+        load_volt(2)
+        mu = []
+        for q in range(NQ):
+            mu_q = keep.tile([P, MU_TILES, L], BF16, name="mu_%d" % q)
+            mu.append(mu_q)
+        nc.sync.dma_start(out=mu[0][:], in_=mu_view[:, 0:MU_TILES, :])
+        load_volt(3)
+        load_volt(4)
+        nc.sync.dma_start(out=mu[1][:], in_=mu_view[:, MU_TILES : 2 * MU_TILES, :])
+        load_volt(5)
+        load_volt(6)
+        nc.sync.dma_start(out=mu[2][:], in_=mu_view[:, 2 * MU_TILES : 3 * MU_TILES, :])
+        load_volt(7)
+        load_volt(8)
+        load_volt(9)
+        nc.sync.dma_start(out=mu[3][:], in_=mu_view[:, 3 * MU_TILES : 4 * MU_TILES, :])
+
+        for r in range(1, 4):
+            nc.scalar.copy(out=scale_rows[:, r, :], in_=scale_rows[:, 0, :])
+
+        im_words = keep.tile([P, 1024], U8, align_bytes=64)
+        im_scales = keep.tile([P, 512], U8, align_bytes=64)
+        nc.vector.tensor_copy(
+            out=im_words[:].rearrange("p (t m e) -> p m t e", t=4, e=2),
+            in_=im_words_raw[:].rearrange("p (m t e) -> p m t e", t=4, e=2),
+        )
+        nc.vector.tensor_copy(
+            out=im_scales[:].rearrange("p (t m) -> p m t", t=4),
+            in_=im_scales_raw[:].rearrange("p (m t) -> p m t", t=4),
+        )
+
+        neg = []
+        for q in range(NQ):
+            neg_q = keep.tile([P, MU_TILES, L], BF16, name="neg_%d" % q)
+            neg.append(neg_q)
+        sq_sums = keep.tile([P, NT], F32)
+        abs_sums = keep.tile([P, NT], F32)
+        neg_sums = keep.tile([P, NT], F32)
+        final = keep.tile([P, NT], F32)
+
+        rows_of, xt_of, grouped_of, xq_of, dv_of, dvg_of, dvq_of, ib_of, sq_of, cur_of, prod_of = ({} for i in range(11))
+
+        def stage_w(u):
+            c0, n = UNITS[u]
+            rows = flow.tile([P, n * K], BF16, tag="rows", name="rows")
+            rows_of[u] = rows
+            t, j = raw_of_tile[c0]
+            src = t[:, j : j + n, :].rearrange("p j k -> p (j k)").bitcast(FP8)
+            if u in CAST_UNITS:
+                if u in CAST_ON_SCALAR:
+                    nc.scalar.copy(out=rows[:], in_=src)
+                else:
+                    nc.vector.tensor_copy(out=rows[:], in_=src)
+            else:
+                nc.vector.tensor_tensor(out=rows[:], in0=src, in1=scale_rows[:, 0:n, :].rearrange("p j k -> p (j k)"), op=ALU.mult)
+
+        def stage_t(u):
+            c0, n = UNITS[u]
+            words = rows_of[u][:].bitcast(F32)
+            for g in range(n // 2):
+                xt = xt_pool.tile([P, 2, 2 * P], F32, tag="xt", name="xt")
+                xt_of[c0 + 2 * g] = xt
+                for i in range(2):
+                    j = 2 * g + i
+                    for h in range(2):
+                        nc.tensor.transpose(xt[:, h, P * i : P * (i + 1)], words[:, 256 * j + h : 256 * (j + 1) : 2], ident_f32[:])
+
+        def stage_e(u):
+            c0, n = UNITS[u]
+            grouped = flow.tile([P, n * K], BF16, tag="grouped", name="grouped", bufs=3, align_bytes=64)
+            grouped_of[u] = grouped
+            for g in range(n // 2):
+                xt = xt_of[c0 + 2 * g]
+                dst = grouped[:, 2 * K * g : 2 * K * (g + 1)]
+                if u in CAST_UNITS:
+                    nc.vector.tensor_tensor(
+                        out=dst.rearrange("p (c h e) -> p c h e", h=2, e=2),
+                        in0=xt[:].bitcast(BF16).rearrange("p h (c e) -> p c h e", e=2),
+                        in1=scale_cols[:].rearrange("p (h e) -> p h e", e=2).unsqueeze(1).to_broadcast([P, 2 * P, 2, 2]),
+                        op=ALU.mult,
+                    )
+                else:
+                    nc.scalar.copy(out=dst.bitcast(F32).rearrange("p (c h) -> p c h", h=2), in_=xt[:].rearrange("p h c -> p c h"))
+
+        def stage_q(u):
+            c0, n = UNITS[u]
+            xq = flow.tile([P, n * P], U32, tag="xq", name="xq", align_bytes=64)
+            xs = flow.tile([P, n * P], U8, tag="xs", name="xs", align_bytes=64)
+            xq_of[u] = (xq, xs)
+            nc.vector.quantize_mx(out=xq[:].bitcast(FP8X4), scales=xs[:], in_=grouped_of[u][:])
+
+        def stage_m1(u):
+            c0, n = UNITS[u]
+            xq, xs = xq_of[u]
+            for j in range(n):
+                dv = dv_pool.tile([P, 4, P], F32, tag="dv", name="dv")
+                dv_of[c0 + j] = dv
+                for t in range(4):
+                    nc.tensor.matmul_mx(
+                        out=dv[:, t, :],
+                        lhsT=im_words[:, 256 * t : 256 * (t + 1)].bitcast(FP4X4),
+                        lhsT_scale=im_scales[:, P * t : P * (t + 1)],
+                        rhs=xq[:, P * j : P * (j + 1)].bitcast(FP8X4),
+                        rhs_scale=xs[:, P * j : P * (j + 1)],
+                        start=True,
+                        stop=True,
+                    )
+
+        def stage_d(u):
+            c0, n = UNITS[u]
+            dvg = flow.tile([P, n * K], BF16, tag="dvg", name="dvg", bufs=3, align_bytes=64)
+            dvg_of[u] = dvg
+            for j in range(n):
+                dst = dvg[:, K * j : K * (j + 1)].rearrange("p (c t) -> p c t", t=4)
+                src = dv_of[c0 + j][:].rearrange("p t c -> p c t")
+                if c0 + j in D_ON_VECTOR:
+                    nc.vector.tensor_copy(out=dst, in_=src)
+                else:
+                    nc.scalar.copy(out=dst, in_=src)
+
+        def stage_r(u):
+            c0, n = UNITS[u]
+            dvq = flow.tile([P, n * P], U32, tag="dvq", name="dvq", align_bytes=64)
+            dvs = flow.tile([P, n * P], U8, tag="dvs", name="dvs", align_bytes=64)
+            dvq_of[u] = (dvq, dvs)
+            nc.vector.quantize_mx(out=dvq[:].bitcast(FP8X4), scales=dvs[:], in_=dvg_of[u][:])
+
+        def stage_m2(u):
+            c0, n = UNITS[u]
+            dvq, dvs = dvq_of[u]
+            for j in range(n):
+                ib = ib_pool.tile([P, 512], F32, tag="ib", name="ib")
+                ib_of[c0 + j] = ib
+                nc.tensor.matmul_mx(
+                    out=ib[:],
+                    lhsT=dvq[:, P * j : P * (j + 1)].bitcast(FP8X4),
+                    lhsT_scale=dvs[:, P * j : P * (j + 1)],
+                    rhs=yb_words[:].bitcast(FP4X4),
+                    rhs_scale=yb_scales[:],
+                    start=True,
+                    stop=True,
+                )
+
+        def stage_f(u):
+            c0, n = UNITS[u]
+            sq = flow.tile([P, n, 512], F32, tag="sq", name="sq", bufs=3)
+            sq_of[u] = sq
+            for j in range(n):
+                c = c0 + j
+                nc.scalar.activation(out=sq[:, j, :], in_=ib_of[c][:], func=ACT.Square, accum_out=sq_sums[:, c : c + 1])
+
+        def stage_a(u):
+            c0, n = UNITS[u]
+            q, i = divmod(c0, MU_TILES)
+            src = mu[q][:, i : i + n, :].rearrange("p j l -> p (j l)")
+            nc.vector.tensor_scalar(
+                out=neg[q][:, i : i + n, :].rearrange("p j l -> p (j l)"), in0=src, scalar1=-1.0, scalar2=0.0, op0=ALU.mult, op1=ALU.max
+            )
+            nc.vector.tensor_scalar(
+                out=src.bitcast(I32),
+                in0=src.bitcast(I32),
+                scalar1=0x7FFF7FFF,
+                scalar2=None,
+                op0=ALU.bitwise_and,
+            )
+
+        def stage_g(u):
+            c0, n = UNITS[u]
+            cur = flow.tile([P, n, L], F32, tag="cur", name="cur", bufs=2)
+            cur_of[u] = cur
+            sq = sq_of[u]
+            nc.vector.scalar_tensor_tensor(out=cur[:], in0=sq[:, :, 0:L], scalar=-1.0, in1=sq[:, :, L : 2 * L], op0=ALU.add, op1=ALU.add)
+
+        def stage_y(u):
+            c0, n = UNITS[u]
+            prod = flow.tile([P, n, L], F32, tag="prod", name="prod", bufs=3)
+            prod_of[u] = prod
+            q, i = divmod(c0, MU_TILES)
+            nc.vector.scalar_tensor_tensor(out=prod[:], in0=mu[q][:, i : i + n, :], scalar=0.5, in1=cur_of[u][:], op0=ALU.add, op1=ALU.mult)
+
+        def stage_b(u):
+            c0, n = UNITS[u]
+            for j in range(n):
+                junk = flow.tile([P, L], F32, tag="junk", name="junk", bufs=2)
+                nc.scalar.activation(out=junk[:], in_=prod_of[u][:, j, :], func=ACT.Abs, accum_out=abs_sums[:, c0 + j : c0 + j + 1])
+
+        def stage_s(u):
+            c0, n = UNITS[u]
+            if (c0 + n) % MU_TILES == 0:
+                q = c0 // MU_TILES
+                acc = ib_pool.tile([P, 512], F32, tag="ib", name="acc")
+                for c in range(8):
+                    nc.tensor.matmul(acc[:], lhsT=ident_bf16[:], rhs=neg[q][:, :, 32 * c : 32 * (c + 1)], start=(c == 0), stop=(c == 7))
+                nc.vector.tensor_reduce(
+                    out=neg_sums[:, MU_TILES * q : MU_TILES * (q + 1)],
+                    in_=acc[:].rearrange("p (j l) -> p j l", l=32),
+                    axis=AX.X,
+                    op=ALU.add,
+                )
+
+        stages = {"W": stage_w, "T": stage_t, "E": stage_e, "Q": stage_q, "M1": stage_m1, "D": stage_d, "R": stage_r, "M2": stage_m2, "F": stage_f, "A": stage_a, "G": stage_g, "Y": stage_y, "B": stage_b, "S": stage_s}
+        deepest = max(lag for name, lag in ORDER)
+        for step in range(NU + deepest):
+            for name, lag in ORDER:
+                if 0 <= step - lag < NU:
+                    stages[name](step - lag)
+
+        nc.vector.scalar_tensor_tensor(out=final[:], in0=sq_sums[:], scalar=0.5, in1=neg_sums[:], op0=ALU.mult, op1=ALU.add)
+        nc.vector.scalar_tensor_tensor(out=final[:], in0=final[:], scalar=-0.5 * L, in1=abs_sums[:], op0=ALU.add, op1=ALU.add)
+        nc.sync.dma_start(out=out.rearrange("(p j) -> p j", p=P), in_=final[:])

@@ -18,7 +18,7 @@ AX = mybir.AxisListType
 B, K, L = 8192, 512, 256
 P = 128
 NT = B // P
-UNIT_SIZES = [2, 2] + [4] * 14 + [2, 2]
+UNIT_SIZES = [2] * 4 + [4] * 13 + [2] * 2
 UNITS = [(sum(UNIT_SIZES[:i]), n) for i, n in enumerate(UNIT_SIZES)]
 NU = len(UNITS)
 FLOPS = 2 * 2 * B * K * K
@@ -27,10 +27,40 @@ VOLT_CHUNKS = [2, 2, 4, 8, 8, 8, 8, 8, 8, 8]
 MU_TILES = 16
 NQ = NT // MU_TILES
 CAST_UNITS = (0, 1)
-CAST_ON_SCALAR = (1,)
-D_ON_VECTOR = tuple(range(9, NT, 10))
+CAST_ON_SCALAR = (0, 1)
+D_ON_VECTOR = (1, 21, 43)
+ABS_ON_VECTOR = (3, 7, 11, 15, 18)
 
-ORDER = (("W", 0), ("T", 0), ("E", 0), ("Q", 0), ("M1", 0), ("A", 0), ("D", 1), ("R", 1), ("M2", 1), ("F", 1), ("G", 2), ("Y", 2), ("B", 2), ("S", 2))
+ORDER = (
+    ("Z", 7),
+    ("D0", 3),
+    ("T0", 1),
+    ("Y", 7),
+    ("D1", 3),
+    ("B0", 10),
+    ("M20", 4),
+    ("D2", 3),
+    ("B1", 10),
+    ("D3", 3),
+    ("E0", 1),
+    ("W", 0),
+    ("T1", 1),
+    ("A", 5),
+    ("R", 3),
+    ("B2", 10),
+    ("B3", 10),
+    ("M10", 2),
+    ("M21", 4),
+    ("S", 6),
+    ("F0", 4),
+    ("M11", 2),
+    ("F1", 4),
+    ("E1", 1),
+    ("Q", 1),
+    ("F2", 4),
+    ("F3", 4),
+    ("G", 5),
+)
 
 
 def tile_pinnlayer_pa_t_w4_kernel(tc, Volt_bytes, Volt_scale, IM_words, IM_scales, Ybr_words, Ybr_scales, n_o_mu_i_u, out):
@@ -99,19 +129,6 @@ def tile_pinnlayer_pa_t_w4_kernel(tc, Volt_bytes, Volt_scale, IM_words, IM_scale
         load_volt(9)
         nc.sync.dma_start(out=mu[3][:], in_=mu_view[:, 3 * MU_TILES : 4 * MU_TILES, :])
 
-        for r in range(1, 4):
-            nc.scalar.copy(out=scale_rows[:, r, :], in_=scale_rows[:, 0, :])
-
-        im_words = keep.tile([P, 1024], U8, align_bytes=64)
-        im_scales = keep.tile([P, 512], U8, align_bytes=64)
-        nc.vector.tensor_copy(
-            out=im_words[:].rearrange("p (t m e) -> p m t e", t=4, e=2),
-            in_=im_words_raw[:].rearrange("p (m t e) -> p m t e", t=4, e=2),
-        )
-        nc.vector.tensor_copy(
-            out=im_scales[:].rearrange("p (t m) -> p m t", t=4),
-            in_=im_scales_raw[:].rearrange("p (m t) -> p m t", t=4),
-        )
 
         neg = []
         for q in range(NQ):
@@ -122,7 +139,7 @@ def tile_pinnlayer_pa_t_w4_kernel(tc, Volt_bytes, Volt_scale, IM_words, IM_scale
         neg_sums = keep.tile([P, NT], F32)
         final = keep.tile([P, NT], F32)
 
-        rows_of, xt_of, grouped_of, xq_of, dv_of, dvg_of, dvq_of, ib_of, sq_of, cur_of, prod_of = ({} for i in range(11))
+        rows_of, xt_of, grouped_of, xq_of, dv_of, dvg_of, dvq_of, ib_of, sq_of, cur_of, acc_of = ({} for i in range(11))
 
         def stage_w(u):
             c0, n = UNITS[u]
@@ -138,10 +155,10 @@ def tile_pinnlayer_pa_t_w4_kernel(tc, Volt_bytes, Volt_scale, IM_words, IM_scale
             else:
                 nc.vector.tensor_tensor(out=rows[:], in0=src, in1=scale_rows[:, 0:n, :].rearrange("p j k -> p (j k)"), op=ALU.mult)
 
-        def stage_t(u):
+        def stage_t(u, g):
             c0, n = UNITS[u]
             words = rows_of[u][:].bitcast(F32)
-            for g in range(n // 2):
+            if 2 * g < n:
                 xt = xt_pool.tile([P, 2, 2 * P], F32, tag="xt", name="xt")
                 xt_of[c0 + 2 * g] = xt
                 for i in range(2):
@@ -149,11 +166,13 @@ def tile_pinnlayer_pa_t_w4_kernel(tc, Volt_bytes, Volt_scale, IM_words, IM_scale
                     for h in range(2):
                         nc.tensor.transpose(xt[:, h, P * i : P * (i + 1)], words[:, 256 * j + h : 256 * (j + 1) : 2], ident_f32[:])
 
-        def stage_e(u):
+        def stage_e(u, g):
             c0, n = UNITS[u]
-            grouped = flow.tile([P, n * K], BF16, tag="grouped", name="grouped", bufs=3, align_bytes=64)
-            grouped_of[u] = grouped
-            for g in range(n // 2):
+            if g == 0:
+                grouped = flow.tile([P, n * K], BF16, tag="grouped", name="grouped", bufs=3, align_bytes=64)
+                grouped_of[u] = grouped
+            grouped = grouped_of[u]
+            if 2 * g < n:
                 xt = xt_of[c0 + 2 * g]
                 dst = grouped[:, 2 * K * g : 2 * K * (g + 1)]
                 if u in CAST_UNITS:
@@ -173,10 +192,10 @@ def tile_pinnlayer_pa_t_w4_kernel(tc, Volt_bytes, Volt_scale, IM_words, IM_scale
             xq_of[u] = (xq, xs)
             nc.vector.quantize_mx(out=xq[:].bitcast(FP8X4), scales=xs[:], in_=grouped_of[u][:])
 
-        def stage_m1(u):
+        def stage_m1(u, g):
             c0, n = UNITS[u]
             xq, xs = xq_of[u]
-            for j in range(n):
+            for j in range(2 * g, min(2 * g + 2, n)):
                 dv = dv_pool.tile([P, 4, P], F32, tag="dv", name="dv")
                 dv_of[c0 + j] = dv
                 for t in range(4):
@@ -190,11 +209,13 @@ def tile_pinnlayer_pa_t_w4_kernel(tc, Volt_bytes, Volt_scale, IM_words, IM_scale
                         stop=True,
                     )
 
-        def stage_d(u):
+        def stage_d(u, half):
             c0, n = UNITS[u]
-            dvg = flow.tile([P, n * K], BF16, tag="dvg", name="dvg", bufs=3, align_bytes=64)
-            dvg_of[u] = dvg
-            for j in range(n):
+            if half == 0:
+                dvg = flow.tile([P, n * K], BF16, tag="dvg", name="dvg", bufs=3, align_bytes=64)
+                dvg_of[u] = dvg
+            dvg = dvg_of[u]
+            for j in range(half, min(half + 1, n)):
                 dst = dvg[:, K * j : K * (j + 1)].rearrange("p (c t) -> p c t", t=4)
                 src = dv_of[c0 + j][:].rearrange("p t c -> p c t")
                 if c0 + j in D_ON_VECTOR:
@@ -209,10 +230,10 @@ def tile_pinnlayer_pa_t_w4_kernel(tc, Volt_bytes, Volt_scale, IM_words, IM_scale
             dvq_of[u] = (dvq, dvs)
             nc.vector.quantize_mx(out=dvq[:].bitcast(FP8X4), scales=dvs[:], in_=dvg_of[u][:])
 
-        def stage_m2(u):
+        def stage_m2(u, g):
             c0, n = UNITS[u]
             dvq, dvs = dvq_of[u]
-            for j in range(n):
+            for j in range(2 * g, min(2 * g + 2, n)):
                 ib = ib_pool.tile([P, 512], F32, tag="ib", name="ib")
                 ib_of[c0 + j] = ib
                 nc.tensor.matmul_mx(
@@ -225,11 +246,13 @@ def tile_pinnlayer_pa_t_w4_kernel(tc, Volt_bytes, Volt_scale, IM_words, IM_scale
                     stop=True,
                 )
 
-        def stage_f(u):
+        def stage_f(u, half):
             c0, n = UNITS[u]
-            sq = flow.tile([P, n, 512], F32, tag="sq", name="sq", bufs=3)
-            sq_of[u] = sq
-            for j in range(n):
+            if half == 0:
+                sq = flow.tile([P, n, 512], F32, tag="sq", name="sq", bufs=3)
+                sq_of[u] = sq
+            sq = sq_of[u]
+            for j in range(half, min(half + 1, n)):
                 c = c0 + j
                 nc.scalar.activation(out=sq[:, j, :], in_=ib_of[c][:], func=ACT.Square, accum_out=sq_sums[:, c : c + 1])
 
@@ -250,23 +273,25 @@ def tile_pinnlayer_pa_t_w4_kernel(tc, Volt_bytes, Volt_scale, IM_words, IM_scale
 
         def stage_g(u):
             c0, n = UNITS[u]
-            cur = flow.tile([P, n, L], F32, tag="cur", name="cur", bufs=2)
+            cur = flow.tile([P, n, L], F32, tag="cur", name="cur", bufs=7)
             cur_of[u] = cur
             sq = sq_of[u]
             nc.vector.scalar_tensor_tensor(out=cur[:], in0=sq[:, :, 0:L], scalar=-1.0, in1=sq[:, :, L : 2 * L], op0=ALU.add, op1=ALU.add)
 
         def stage_y(u):
             c0, n = UNITS[u]
-            prod = flow.tile([P, n, L], F32, tag="prod", name="prod", bufs=3)
-            prod_of[u] = prod
+            cur = cur_of[u]
             q, i = divmod(c0, MU_TILES)
-            nc.vector.scalar_tensor_tensor(out=prod[:], in0=mu[q][:, i : i + n, :], scalar=0.5, in1=cur_of[u][:], op0=ALU.add, op1=ALU.mult)
+            nc.vector.scalar_tensor_tensor(out=cur[:], in0=mu[q][:, i : i + n, :], scalar=0.5, in1=cur[:], op0=ALU.add, op1=ALU.mult)
 
-        def stage_b(u):
+        def stage_b(u, j):
             c0, n = UNITS[u]
-            for j in range(n):
+            if u in ABS_ON_VECTOR:
+                if j == 0:
+                    nc.vector.tensor_reduce(out=abs_sums[:, c0 : c0 + n], in_=cur_of[u][:], axis=AX.X, op=ALU.add, apply_absolute_value=True)
+            elif j < n:
                 junk = flow.tile([P, L], F32, tag="junk", name="junk", bufs=2)
-                nc.scalar.activation(out=junk[:], in_=prod_of[u][:, j, :], func=ACT.Abs, accum_out=abs_sums[:, c0 + j : c0 + j + 1])
+                nc.scalar.activation(out=junk[:], in_=cur_of[u][:, j, :], func=ACT.Abs, accum_out=abs_sums[:, c0 + j : c0 + j + 1])
 
         def stage_s(u):
             c0, n = UNITS[u]
@@ -275,6 +300,13 @@ def tile_pinnlayer_pa_t_w4_kernel(tc, Volt_bytes, Volt_scale, IM_words, IM_scale
                 acc = ib_pool.tile([P, 512], F32, tag="ib", name="acc")
                 for c in range(8):
                     nc.tensor.matmul(acc[:], lhsT=ident_bf16[:], rhs=neg[q][:, :, 32 * c : 32 * (c + 1)], start=(c == 0), stop=(c == 7))
+                acc_of[q] = acc
+
+        def stage_z(u):
+            c0, n = UNITS[u]
+            if (c0 + n) % MU_TILES == 0:
+                q = c0 // MU_TILES
+                acc = acc_of[q]
                 nc.vector.tensor_reduce(
                     out=neg_sums[:, MU_TILES * q : MU_TILES * (q + 1)],
                     in_=acc[:].rearrange("p (j l) -> p j l", l=32),
@@ -282,12 +314,40 @@ def tile_pinnlayer_pa_t_w4_kernel(tc, Volt_bytes, Volt_scale, IM_words, IM_scale
                     op=ALU.add,
                 )
 
-        stages = {"W": stage_w, "T": stage_t, "E": stage_e, "Q": stage_q, "M1": stage_m1, "D": stage_d, "R": stage_r, "M2": stage_m2, "F": stage_f, "A": stage_a, "G": stage_g, "Y": stage_y, "B": stage_b, "S": stage_s}
+        stages = {"W": stage_w, "Q": stage_q, "R": stage_r, "A": stage_a, "G": stage_g, "Y": stage_y, "S": stage_s, "Z": stage_z}
+        for g in range(2):
+            stages["T%d" % g] = lambda u, g=g: stage_t(u, g)
+            stages["E%d" % g] = lambda u, g=g: stage_e(u, g)
+            stages["M1%d" % g] = lambda u, g=g: stage_m1(u, g)
+            stages["M2%d" % g] = lambda u, g=g: stage_m2(u, g)
+        for j in range(4):
+            stages["D%d" % j] = lambda u, j=j: stage_d(u, j)
+            stages["F%d" % j] = lambda u, j=j: stage_f(u, j)
+            stages["B%d" % j] = lambda u, j=j: stage_b(u, j)
         deepest = max(lag for name, lag in ORDER)
-        for step in range(NU + deepest):
-            for name, lag in ORDER:
-                if 0 <= step - lag < NU:
-                    stages[name](step - lag)
+        im_words = keep.tile([P, 1024], U8, align_bytes=64)
+        im_scales = keep.tile([P, 512], U8, align_bytes=64)
+
+        def permute_im():
+            nc.vector.tensor_copy(
+                out=im_words[:].rearrange("p (t m e) -> p m t e", t=4, e=2),
+                in_=im_words_raw[:].rearrange("p (m t e) -> p m t e", t=4, e=2),
+            )
+            nc.vector.tensor_copy(
+                out=im_scales[:].rearrange("p (t m) -> p m t", t=4),
+                in_=im_scales_raw[:].rearrange("p (m t) -> p m t", t=4),
+            )
+
+        with tc.manual_schedule(engines={mybir.EngineType.PE, mybir.EngineType.Activation, mybir.EngineType.DVE}):
+            for step in range(NU + deepest):
+                for name, lag in ORDER:
+                    if 0 <= step - lag < NU:
+                        stages[name](step - lag)
+                    if step == 0 and name == "W":
+                        permute_im()
+                    if step == 1 and name == "W":
+                        for r in range(1, 4):
+                            nc.scalar.copy(out=scale_rows[:, r, :], in_=scale_rows[:, 0, :])
 
         nc.vector.scalar_tensor_tensor(out=final[:], in0=sq_sums[:], scalar=0.5, in1=neg_sums[:], op0=ALU.mult, op1=ALU.add)
         nc.vector.scalar_tensor_tensor(out=final[:], in0=final[:], scalar=-0.5 * L, in1=abs_sums[:], op0=ALU.add, op1=ALU.add)

@@ -27,39 +27,39 @@ VOLT_CHUNKS = [2, 2, 4, 8, 8, 8, 8, 8, 8, 8]
 MU_TILES = 16
 NQ = NT // MU_TILES
 CAST_UNITS = (0, 1)
-CAST_ON_SCALAR = (0, 1)
-D_ON_VECTOR = (1, 21, 43)
+CAST_ON_SCALAR = (1,)
+D_ON_VECTOR = (1, 11, 22, 33, 43, 53)
 ABS_ON_VECTOR = (3, 7, 11, 15, 18)
 
 ORDER = (
-    ("Z", 7),
     ("D0", 3),
-    ("T0", 1),
-    ("Y", 7),
     ("D1", 3),
-    ("B0", 10),
+    ("T0", 1),
+    ("B2", 10),
     ("M20", 4),
+    ("B0", 10),
+    ("W", 0),
     ("D2", 3),
-    ("B1", 10),
     ("D3", 3),
     ("E0", 1),
-    ("W", 0),
     ("T1", 1),
-    ("A", 5),
-    ("R", 3),
-    ("B2", 10),
-    ("B3", 10),
-    ("M10", 2),
     ("M21", 4),
-    ("S", 6),
     ("F0", 4),
-    ("M11", 2),
+    ("Y", 7),
+    ("M10", 2),
+    ("Z", 9),
     ("F1", 4),
-    ("E1", 1),
-    ("Q", 1),
-    ("F2", 4),
-    ("F3", 4),
+    ("B1", 10),
+    ("A", 3),
+    ("S", 8),
+    ("B3", 10),
     ("G", 5),
+    ("E1", 1),
+    ("R", 3),
+    ("F2", 4),
+    ("M11", 2),
+    ("F3", 4),
+    ("Q", 1),
 )
 
 
@@ -70,7 +70,8 @@ def tile_pinnlayer_pa_t_w4_kernel(tc, Volt_bytes, Volt_scale, IM_words, IM_scale
         flow = ctx.enter_context(tc.tile_pool(name="flow", bufs=4))
         xt_pool = ctx.enter_context(tc.psum_pool(name="xt_pool", bufs=2))
         dv_pool = ctx.enter_context(tc.psum_pool(name="dv_pool", bufs=3))
-        ib_pool = ctx.enter_context(tc.psum_pool(name="ib_pool", bufs=3))
+        ib_pool = ctx.enter_context(tc.psum_pool(name="ib_pool", bufs=2))
+        acc_pool = ctx.enter_context(tc.psum_pool(name="acc_pool", bufs=1))
 
         volt_view = Volt_bytes.rearrange("(p j) k -> p j k", p=P)
         mu_view = n_o_mu_i_u.rearrange("(p j) l -> p j l", p=P)
@@ -295,12 +296,12 @@ def tile_pinnlayer_pa_t_w4_kernel(tc, Volt_bytes, Volt_scale, IM_words, IM_scale
 
         def stage_s(u):
             c0, n = UNITS[u]
-            if (c0 + n) % MU_TILES == 0:
-                q = c0 // MU_TILES
-                acc = ib_pool.tile([P, 512], F32, tag="ib", name="acc")
-                for c in range(8):
-                    nc.tensor.matmul(acc[:], lhsT=ident_bf16[:], rhs=neg[q][:, :, 32 * c : 32 * (c + 1)], start=(c == 0), stop=(c == 7))
+            q, i = divmod(c0, MU_TILES)
+            if i == 0:
+                acc = acc_pool.tile([P, 512], F32, tag="acc", name="acc")
                 acc_of[q] = acc
+            for c in range(i // 2, (i + n) // 2):
+                nc.tensor.matmul(acc_of[q][:], lhsT=ident_bf16[:], rhs=neg[q][:, :, 32 * c : 32 * (c + 1)], start=(c == 0), stop=(c == 7))
 
         def stage_z(u):
             c0, n = UNITS[u]
@@ -343,7 +344,7 @@ def tile_pinnlayer_pa_t_w4_kernel(tc, Volt_bytes, Volt_scale, IM_words, IM_scale
                 for name, lag in ORDER:
                     if 0 <= step - lag < NU:
                         stages[name](step - lag)
-                    if step == 0 and name == "W":
+                    if step == 1 and name == "W":
                         permute_im()
                     if step == 1 and name == "W":
                         for r in range(1, 4):

@@ -24,43 +24,49 @@ NU = len(UNITS)
 FLOPS = 2 * 2 * B * K * K
 
 VOLT_CHUNKS = [2, 2, 4, 8, 8, 8, 8, 8, 8, 8]
-MU_TILES = 16
-NQ = NT // MU_TILES
-CAST_UNITS = (0, 1)
-CAST_ON_SCALAR = (1,)
-D_ON_VECTOR = (1, 11, 22, 33, 43, 53)
-ABS_ON_VECTOR = (3, 7, 11, 15, 18)
+HALF = NT // 2
+PIECE = 8
+CAST_UNITS = (0, 1, 2)
+CAST_ON_SCALAR = (1, 2)
+D_ON_VECTOR = ()
+ABS_ON_VECTOR = (1, 3, 4, 6, 7, 9, 11, 12, 14, 15, 17, 18)
 
 ORDER = (
     ("D0", 3),
     ("D1", 3),
     ("T0", 1),
-    ("B2", 10),
     ("M20", 4),
-    ("B0", 10),
-    ("W", 0),
     ("D2", 3),
+    ("B0", 9),
+    ("Y", 6),
     ("D3", 3),
-    ("E0", 1),
     ("T1", 1),
-    ("M21", 4),
-    ("F0", 4),
-    ("Y", 7),
-    ("M10", 2),
-    ("Z", 9),
-    ("F1", 4),
-    ("B1", 10),
-    ("A", 3),
-    ("S", 8),
-    ("B3", 10),
+    ("B3", 9),
     ("G", 5),
-    ("E1", 1),
+    ("W", 0),
+    ("E0", 1),
+    ("F0", 4),
+    ("F1", 4),
     ("R", 3),
+    ("S", None),
+    ("B1", 9),
+    ("B2", 9),
+    ("Z", None),
+    ("E1", 1),
+    ("M21", 4),
+    ("A", None),
+    ("M10", 2),
     ("F2", 4),
-    ("M11", 2),
     ("F3", 4),
     ("Q", 1),
+    ("M11", 2),
 )
+A_STEPS = {2 + 2 * k: k for k in range(8)}
+S_STEPS = {
+    **{9 + s: [(0, 4 * s + r) for r in range(4)] for s in range(8)},
+    **{18 + s: [(1, 2 * s + r) for r in range(2)] for s in range(8)},
+}
+Z_STEPS = {17: 0, 26: 1}
 
 
 def tile_pinnlayer_pa_t_w4_kernel(tc, Volt_bytes, Volt_scale, IM_words, IM_scales, Ybr_words, Ybr_scales, n_o_mu_i_u, out):
@@ -115,26 +121,37 @@ def tile_pinnlayer_pa_t_w4_kernel(tc, Volt_bytes, Volt_scale, IM_words, IM_scale
             nc.sync.dma_start(out=yb_scales[32 * q : 32 * q + 4, :].bitcast(I32), in_=Ybr_scales[0, 4 * q : 4 * q + 4, :].bitcast(I32))
         load_volt(2)
         mu = []
-        for q in range(NQ):
-            mu_q = keep.tile([P, MU_TILES, L], BF16, name="mu_%d" % q)
-            mu.append(mu_q)
-        nc.sync.dma_start(out=mu[0][:], in_=mu_view[:, 0:MU_TILES, :])
+        for h in range(2):
+            mu_h = keep.tile([P, HALF, L], BF16, name="mu_%d" % h)
+            mu.append(mu_h)
+
+        def load_mu(k):
+            h, i = divmod(PIECE * k, HALF)
+            nc.sync.dma_start(out=mu[h][:, i : i + PIECE, :], in_=mu_view[:, PIECE * k : PIECE * (k + 1), :])
+
+        load_mu(0)
         load_volt(3)
+        load_mu(1)
         load_volt(4)
-        nc.sync.dma_start(out=mu[1][:], in_=mu_view[:, MU_TILES : 2 * MU_TILES, :])
         load_volt(5)
+        load_mu(2)
         load_volt(6)
-        nc.sync.dma_start(out=mu[2][:], in_=mu_view[:, 2 * MU_TILES : 3 * MU_TILES, :])
+        load_mu(3)
         load_volt(7)
+        load_mu(4)
         load_volt(8)
+        load_mu(5)
         load_volt(9)
-        nc.sync.dma_start(out=mu[3][:], in_=mu_view[:, 3 * MU_TILES : 4 * MU_TILES, :])
+        load_mu(6)
+        load_mu(7)
 
-
-        neg = []
-        for q in range(NQ):
-            neg_q = keep.tile([P, MU_TILES, L], BF16, name="neg_%d" % q)
-            neg.append(neg_q)
+        mag_0 = keep.tile([P, HALF, L], BF16)
+        neg_1 = keep.tile([P, HALF, L], BF16)
+        mag = (mag_0, mu[1])
+        plus_half = keep.tile([P, P], BF16)
+        minus_half = keep.tile([P, P], BF16)
+        nc.vector.tensor_scalar(out=plus_half[:], in0=ident_bf16[:], scalar1=0.5, scalar2=None, op0=ALU.mult)
+        nc.vector.tensor_scalar(out=minus_half[:], in0=ident_bf16[:], scalar1=-0.5, scalar2=None, op0=ALU.mult)
         sq_sums = keep.tile([P, NT], F32)
         abs_sums = keep.tile([P, NT], F32)
         neg_sums = keep.tile([P, NT], F32)
@@ -257,24 +274,26 @@ def tile_pinnlayer_pa_t_w4_kernel(tc, Volt_bytes, Volt_scale, IM_words, IM_scale
                 c = c0 + j
                 nc.scalar.activation(out=sq[:, j, :], in_=ib_of[c][:], func=ACT.Square, accum_out=sq_sums[:, c : c + 1])
 
-        def stage_a(u):
-            c0, n = UNITS[u]
-            q, i = divmod(c0, MU_TILES)
-            src = mu[q][:, i : i + n, :].rearrange("p j l -> p (j l)")
-            nc.vector.tensor_scalar(
-                out=neg[q][:, i : i + n, :].rearrange("p j l -> p (j l)"), in0=src, scalar1=-1.0, scalar2=0.0, op0=ALU.mult, op1=ALU.max
-            )
-            nc.vector.tensor_scalar(
-                out=src.bitcast(I32),
-                in0=src.bitcast(I32),
-                scalar1=0x7FFF7FFF,
-                scalar2=None,
-                op0=ALU.bitwise_and,
-            )
+        def stage_a(step):
+            if step in A_STEPS:
+                h, i = divmod(PIECE * A_STEPS[step], HALF)
+                sel = slice(i, i + PIECE)
+                src = mu[h][:, sel, :].rearrange("p j l -> p (j l)")
+                if h == 1:
+                    nc.vector.tensor_scalar(
+                        out=neg_1[:, sel, :].rearrange("p j l -> p (j l)"), in0=src, scalar1=-1.0, scalar2=0.0, op0=ALU.mult, op1=ALU.max
+                    )
+                nc.vector.tensor_scalar(
+                    out=mag[h][:, sel, :].rearrange("p j l -> p (j l)").bitcast(I32),
+                    in0=src.bitcast(I32),
+                    scalar1=0x7FFF7FFF,
+                    scalar2=None,
+                    op0=ALU.bitwise_and,
+                )
 
         def stage_g(u):
             c0, n = UNITS[u]
-            cur = flow.tile([P, n, L], F32, tag="cur", name="cur", bufs=7)
+            cur = flow.tile([P, n, L], F32, tag="cur", name="cur", bufs=6)
             cur_of[u] = cur
             sq = sq_of[u]
             nc.vector.scalar_tensor_tensor(out=cur[:], in0=sq[:, :, 0:L], scalar=-1.0, in1=sq[:, :, L : 2 * L], op0=ALU.add, op1=ALU.add)
@@ -282,8 +301,8 @@ def tile_pinnlayer_pa_t_w4_kernel(tc, Volt_bytes, Volt_scale, IM_words, IM_scale
         def stage_y(u):
             c0, n = UNITS[u]
             cur = cur_of[u]
-            q, i = divmod(c0, MU_TILES)
-            nc.vector.scalar_tensor_tensor(out=cur[:], in0=mu[q][:, i : i + n, :], scalar=0.5, in1=cur[:], op0=ALU.add, op1=ALU.mult)
+            h, i = divmod(c0, HALF)
+            nc.vector.scalar_tensor_tensor(out=cur[:], in0=mag[h][:, i : i + n, :], scalar=0.5, in1=cur[:], op0=ALU.add, op1=ALU.mult)
 
         def stage_b(u, j):
             c0, n = UNITS[u]
@@ -294,23 +313,27 @@ def tile_pinnlayer_pa_t_w4_kernel(tc, Volt_bytes, Volt_scale, IM_words, IM_scale
                 junk = flow.tile([P, L], F32, tag="junk", name="junk", bufs=2)
                 nc.scalar.activation(out=junk[:], in_=cur_of[u][:, j, :], func=ACT.Abs, accum_out=abs_sums[:, c0 + j : c0 + j + 1])
 
-        def stage_s(u):
-            c0, n = UNITS[u]
-            q, i = divmod(c0, MU_TILES)
-            if i == 0:
-                acc = acc_pool.tile([P, 512], F32, tag="acc", name="acc")
-                acc_of[q] = acc
-            for c in range(i // 2, (i + n) // 2):
-                nc.tensor.matmul(acc_of[q][:], lhsT=ident_bf16[:], rhs=neg[q][:, :, 32 * c : 32 * (c + 1)], start=(c == 0), stop=(c == 7))
+        def stage_s(step):
+            for h, i in S_STEPS.get(step, ()):
+                last = 31 if h == 0 else 15
+                if i == 0:
+                    acc = acc_pool.tile([P, 512], F32, tag="acc", name="acc")
+                    acc_of[h] = acc
+                if h == 1:
+                    weights, values = ident_bf16, neg_1
+                elif i < 16:
+                    weights, values = plus_half, mag[0]
+                else:
+                    weights, values = minus_half, mu[0]
+                c = i % 16
+                nc.tensor.matmul(acc_of[h][:], lhsT=weights[:], rhs=values[:, :, 16 * c : 16 * (c + 1)], start=(i == 0), stop=(i == last))
 
-        def stage_z(u):
-            c0, n = UNITS[u]
-            if (c0 + n) % MU_TILES == 0:
-                q = c0 // MU_TILES
-                acc = acc_of[q]
+        def stage_z(step):
+            if step in Z_STEPS:
+                h = Z_STEPS[step]
                 nc.vector.tensor_reduce(
-                    out=neg_sums[:, MU_TILES * q : MU_TILES * (q + 1)],
-                    in_=acc[:].rearrange("p (j l) -> p j l", l=32),
+                    out=neg_sums[:, HALF * h : HALF * (h + 1)],
+                    in_=acc_of[h][:].rearrange("p (j l) -> p j l", l=16),
                     axis=AX.X,
                     op=ALU.add,
                 )
@@ -325,7 +348,7 @@ def tile_pinnlayer_pa_t_w4_kernel(tc, Volt_bytes, Volt_scale, IM_words, IM_scale
             stages["D%d" % j] = lambda u, j=j: stage_d(u, j)
             stages["F%d" % j] = lambda u, j=j: stage_f(u, j)
             stages["B%d" % j] = lambda u, j=j: stage_b(u, j)
-        deepest = max(lag for name, lag in ORDER)
+        deepest = max(lag for name, lag in ORDER if lag is not None)
         im_words = keep.tile([P, 1024], U8, align_bytes=64)
         im_scales = keep.tile([P, 512], U8, align_bytes=64)
 
@@ -342,11 +365,13 @@ def tile_pinnlayer_pa_t_w4_kernel(tc, Volt_bytes, Volt_scale, IM_words, IM_scale
         with tc.manual_schedule(engines={mybir.EngineType.PE, mybir.EngineType.Activation, mybir.EngineType.DVE}):
             for step in range(NU + deepest):
                 for name, lag in ORDER:
-                    if 0 <= step - lag < NU:
+                    if lag is None:
+                        stages[name](step)
+                    elif 0 <= step - lag < NU:
                         stages[name](step - lag)
-                    if step == 1 and name == "W":
+                    if step == 0 and name == "W":
                         permute_im()
-                    if step == 1 and name == "W":
+                    if step == 2 and name == "W":
                         for r in range(1, 4):
                             nc.scalar.copy(out=scale_rows[:, r, :], in_=scale_rows[:, 0, :])
 

@@ -18,7 +18,7 @@ AX = mybir.AxisListType
 B, K, L = 8192, 512, 256
 P = 128
 NT = B // P
-UNIT_SIZES = [2] * 4 + [4] * 13 + [2] * 2
+UNIT_SIZES = [2] * 4 + [4] * 12 + [2] * 4
 UNITS = [(sum(UNIT_SIZES[:i]), n) for i, n in enumerate(UNIT_SIZES)]
 NU = len(UNITS)
 FLOPS = 2 * 2 * B * K * K
@@ -29,44 +29,47 @@ PIECE = 8
 CAST_UNITS = (0, 1, 2)
 CAST_ON_SCALAR = (1, 2)
 D_ON_VECTOR = ()
-ABS_ON_VECTOR = (1, 3, 4, 6, 7, 9, 11, 12, 14, 15, 17, 18)
+ABS_ON_VECTOR = (0, 2, 3, 5, 6, 7, 9, 10, 11, 14, 18, 19)
+
+AHEAD_UNITS = tuple(range(1, 3))
 
 ORDER = (
-    ("D0", 3),
-    ("D1", 3),
-    ("T0", 1),
-    ("M20", 4),
-    ("D2", 3),
-    ("B0", 9),
-    ("Y", 6),
-    ("D3", 3),
-    ("T1", 1),
-    ("B3", 9),
-    ("G", 5),
-    ("W", 0),
-    ("E0", 1),
-    ("F0", 4),
-    ("F1", 4),
-    ("R", 3),
-    ("S", None),
-    ("B1", 9),
-    ("B2", 9),
     ("Z", None),
+    ("W", 0),
+    ("M20", 5),
+    ("D0", 3),
+    ("T0", 1),
+    ("T1", 1),
+    ("B0", 10),
+    ("S", None),
+    ("D1", 3),
+    ("D2", 3),
+    ("F0", 5),
+    ("M21", 5),
+    ("F1", 5),
+    ("E0", 1),
+    ("G", 6),
     ("E1", 1),
-    ("M21", 4),
-    ("A", None),
-    ("M10", 2),
-    ("F2", 4),
-    ("F3", 4),
+    ("B2", 10),
+    ("D3", 3),
+    ("R", 3),
     ("Q", 1),
+    ("A", None),
+    ("B1", 10),
+    ("B3", 10),
+    ("F2", 5),
+    ("Y", 7),
+    ("M10", 2),
     ("M11", 2),
+    ("F3", 5),
 )
-A_STEPS = {2 + 2 * k: k for k in range(8)}
+LAG = {name: lag for name, lag in ORDER}
+A_STEPS = {4 + 1 * k: k for k in range(0, 8)}
 S_STEPS = {
-    **{9 + s: [(0, 4 * s + r) for r in range(4)] for s in range(8)},
-    **{18 + s: [(1, 2 * s + r) for r in range(2)] for s in range(8)},
+    **{8 + s: [(0, i) for i in range(4 * s, min(4 * s + 4, 32))] for s in range(8)},
+    **{17 + s: [(1, i) for i in range(2 * s, min(2 * s + 2, 16))] for s in range(8)},
 }
-Z_STEPS = {17: 0, 26: 1}
+Z_STEPS = {16: 0, 25: 1}
 
 
 def tile_pinnlayer_pa_t_w4_kernel(tc, Volt_bytes, Volt_scale, IM_words, IM_scales, Ybr_words, Ybr_scales, n_o_mu_i_u, out):
@@ -105,21 +108,6 @@ def tile_pinnlayer_pa_t_w4_kernel(tc, Volt_bytes, Volt_scale, IM_words, IM_scale
             t, first, n = chunks[i]
             nc.sync.dma_start(out=t[:], in_=volt_view[:, first : first + n, :])
 
-        load_volt(0)
-        scale_cols = keep.tile([P, 4], F32)
-        nc.sync.dma_start(out=scale_cols[:], in_=Volt_scale.rearrange("o (p t) -> p (o t)", t=4))
-        im_words_raw = keep.tile([P, 1024], U8)
-        nc.sync.dma_start(out=im_words_raw[:], in_=IM_words[0])
-        for q in range(4):
-            nc.sync.dma_start(out=im_scales_raw[32 * q : 32 * q + 4, :].bitcast(I32), in_=IM_scales[0, 4 * q : 4 * q + 4, :].bitcast(I32))
-        load_volt(1)
-        scale_rows = keep.tile([P, 4, K], F32)
-        nc.sync.dma_start(out=scale_rows[:, 0, :], in_=Volt_scale.rearrange("o k -> (o k)").partition_broadcast(P))
-        yb_words = keep.tile([P, 1024], U8, align_bytes=64)
-        nc.sync.dma_start(out=yb_words[:], in_=Ybr_words[0])
-        for q in range(4):
-            nc.sync.dma_start(out=yb_scales[32 * q : 32 * q + 4, :].bitcast(I32), in_=Ybr_scales[0, 4 * q : 4 * q + 4, :].bitcast(I32))
-        load_volt(2)
         mu = []
         for h in range(2):
             mu_h = keep.tile([P, HALF, L], BF16, name="mu_%d" % h)
@@ -129,6 +117,21 @@ def tile_pinnlayer_pa_t_w4_kernel(tc, Volt_bytes, Volt_scale, IM_words, IM_scale
             h, i = divmod(PIECE * k, HALF)
             nc.sync.dma_start(out=mu[h][:, i : i + PIECE, :], in_=mu_view[:, PIECE * k : PIECE * (k + 1), :])
 
+        load_volt(0)
+        scale_cols = keep.tile([P, 4], F32)
+        nc.sync.dma_start(out=scale_cols[:], in_=Volt_scale.rearrange("o (p t) -> p (o t)", t=4))
+        im_words_raw = keep.tile([P, 1024], U8)
+        nc.sync.dma_start(out=im_words_raw[:], in_=IM_words[0])
+        for q in range(4):
+            nc.sync.dma_start(out=im_scales_raw[32 * q : 32 * q + 4, :].bitcast(I32), in_=IM_scales[0, 4 * q : 4 * q + 4, :].bitcast(I32))
+        load_volt(1)
+        load_volt(2)
+        scale_rows = keep.tile([P, 4, K], F32)
+        nc.sync.dma_start(out=scale_rows[:, 0, :], in_=Volt_scale.rearrange("o k -> (o k)").partition_broadcast(P))
+        yb_words = keep.tile([P, 1024], U8, align_bytes=64)
+        nc.sync.dma_start(out=yb_words[:], in_=Ybr_words[0])
+        for q in range(4):
+            nc.sync.dma_start(out=yb_scales[32 * q : 32 * q + 4, :].bitcast(I32), in_=Ybr_scales[0, 4 * q : 4 * q + 4, :].bitcast(I32))
         load_mu(0)
         load_volt(3)
         load_mu(1)
@@ -157,7 +160,7 @@ def tile_pinnlayer_pa_t_w4_kernel(tc, Volt_bytes, Volt_scale, IM_words, IM_scale
         neg_sums = keep.tile([P, NT], F32)
         final = keep.tile([P, NT], F32)
 
-        rows_of, xt_of, grouped_of, xq_of, dv_of, dvg_of, dvq_of, ib_of, sq_of, cur_of, acc_of = ({} for i in range(11))
+        rows_of, xt_of, plain_of, quant_of, dv_of, ib_of, sq_of, cur_of, acc_of = ({} for i in range(9))
 
         def stage_w(u):
             c0, n = UNITS[u]
@@ -186,13 +189,9 @@ def tile_pinnlayer_pa_t_w4_kernel(tc, Volt_bytes, Volt_scale, IM_words, IM_scale
 
         def stage_e(u, g):
             c0, n = UNITS[u]
-            if g == 0:
-                grouped = flow.tile([P, n * K], BF16, tag="grouped", name="grouped", bufs=3, align_bytes=64)
-                grouped_of[u] = grouped
-            grouped = grouped_of[u]
             if 2 * g < n:
                 xt = xt_of[c0 + 2 * g]
-                dst = grouped[:, 2 * K * g : 2 * K * (g + 1)]
+                dst = plain_tile(u + LAG["Q"])[:, 2 * K * g : 2 * K * (g + 1)]
                 if u in CAST_UNITS:
                     nc.vector.tensor_tensor(
                         out=dst.rearrange("p (c h e) -> p c h e", h=2, e=2),
@@ -203,16 +202,40 @@ def tile_pinnlayer_pa_t_w4_kernel(tc, Volt_bytes, Volt_scale, IM_words, IM_scale
                 else:
                     nc.scalar.copy(out=dst.bitcast(F32).rearrange("p (c h) -> p c h", h=2), in_=xt[:].rearrange("p h c -> p c h"))
 
+        def widths(step):
+            u, v = step - LAG["Q"], step - LAG["R"]
+            return (UNITS[u][1] if 0 <= u < NU else 0), (UNITS[v][1] if 0 <= v < NU else 0)
+
+        def plain_tile(step):
+            if step not in plain_of:
+                m, n = widths(step)
+                plain = flow.tile([P, (m + n) * K], BF16, tag="plain", name="plain", bufs=3, align_bytes=64)
+                plain_of[step] = plain
+                codes = flow.tile([P, (m + n) * P], U32, tag="codes", name="codes", bufs=3, align_bytes=64)
+                scales = flow.tile([P, (m + n) * P], U8, tag="scales", name="scales", bufs=3, align_bytes=64)
+                quant_of[step] = (codes, scales)
+            return plain_of[step]
+
+        def quantise(step, first, last):
+            codes, scales = quant_of[step]
+            nc.vector.quantize_mx(
+                out=codes[:, P * first : P * last].bitcast(FP8X4),
+                scales=scales[:, P * first : P * last],
+                in_=plain_of[step][:, K * first : K * last],
+            )
+
         def stage_q(u):
-            c0, n = UNITS[u]
-            xq = flow.tile([P, n * P], U32, tag="xq", name="xq", align_bytes=64)
-            xs = flow.tile([P, n * P], U8, tag="xs", name="xs", align_bytes=64)
-            xq_of[u] = (xq, xs)
-            nc.vector.quantize_mx(out=xq[:].bitcast(FP8X4), scales=xs[:], in_=grouped_of[u][:])
+            m, n = widths(u + LAG["Q"])
+            quantise(u + LAG["Q"], 0, m + n if m + n in (2, 4, 8) else m)
+
+        def stage_r(u):
+            m, n = widths(u + LAG["R"])
+            if m == 0 or m + n not in (2, 4, 8):
+                quantise(u + LAG["R"], m, m + n)
 
         def stage_m1(u, g):
             c0, n = UNITS[u]
-            xq, xs = xq_of[u]
+            xq, xs = quant_of[u + LAG["Q"]]
             for j in range(2 * g, min(2 * g + 2, n)):
                 dv = dv_pool.tile([P, 4, P], F32, tag="dv", name="dv")
                 dv_of[c0 + j] = dv
@@ -229,28 +252,20 @@ def tile_pinnlayer_pa_t_w4_kernel(tc, Volt_bytes, Volt_scale, IM_words, IM_scale
 
         def stage_d(u, half):
             c0, n = UNITS[u]
-            if half == 0:
-                dvg = flow.tile([P, n * K], BF16, tag="dvg", name="dvg", bufs=3, align_bytes=64)
-                dvg_of[u] = dvg
-            dvg = dvg_of[u]
+            m, n = widths(u + LAG["R"])
             for j in range(half, min(half + 1, n)):
-                dst = dvg[:, K * j : K * (j + 1)].rearrange("p (c t) -> p c t", t=4)
+                dst = plain_tile(u + LAG["R"])[:, K * (m + j) : K * (m + j + 1)].rearrange("p (c t) -> p c t", t=4)
                 src = dv_of[c0 + j][:].rearrange("p t c -> p c t")
                 if c0 + j in D_ON_VECTOR:
                     nc.vector.tensor_copy(out=dst, in_=src)
                 else:
                     nc.scalar.copy(out=dst, in_=src)
 
-        def stage_r(u):
-            c0, n = UNITS[u]
-            dvq = flow.tile([P, n * P], U32, tag="dvq", name="dvq", align_bytes=64)
-            dvs = flow.tile([P, n * P], U8, tag="dvs", name="dvs", align_bytes=64)
-            dvq_of[u] = (dvq, dvs)
-            nc.vector.quantize_mx(out=dvq[:].bitcast(FP8X4), scales=dvs[:], in_=dvg_of[u][:])
-
         def stage_m2(u, g):
             c0, n = UNITS[u]
-            dvq, dvs = dvq_of[u]
+            codes, scales = quant_of[u + LAG["R"]]
+            m, n = widths(u + LAG["R"])
+            dvq, dvs = codes[:, P * m : P * (m + n)], scales[:, P * m : P * (m + n)]
             for j in range(2 * g, min(2 * g + 2, n)):
                 ib = ib_pool.tile([P, 512], F32, tag="ib", name="ib")
                 ib_of[c0 + j] = ib
@@ -367,13 +382,18 @@ def tile_pinnlayer_pa_t_w4_kernel(tc, Volt_bytes, Volt_scale, IM_words, IM_scale
                 for name, lag in ORDER:
                     if lag is None:
                         stages[name](step)
-                    elif 0 <= step - lag < NU:
+                    elif 0 <= step - lag < NU and not (name == "W" and step in AHEAD_UNITS):
                         stages[name](step - lag)
-                    if step == 0 and name == "W":
-                        permute_im()
-                    if step == 2 and name == "W":
-                        for r in range(1, 4):
-                            nc.scalar.copy(out=scale_rows[:, r, :], in_=scale_rows[:, 0, :])
+                    if name == "W":
+                        if step == 1:
+                            permute_im()
+                        if step == 0:
+                            for u in AHEAD_UNITS:
+                                stage_w(u)
+                        if step == 2:
+                            nc.scalar.copy(out=scale_rows[:, 1, :], in_=scale_rows[:, 0, :])
+                        if step == 3:
+                            nc.scalar.copy(out=scale_rows[:, 2:4, :], in_=scale_rows[:, 0:2, :])
 
         nc.vector.scalar_tensor_tensor(out=final[:], in0=sq_sums[:], scalar=0.5, in1=neg_sums[:], op0=ALU.mult, op1=ALU.add)
         nc.vector.scalar_tensor_tensor(out=final[:], in0=final[:], scalar=-0.5 * L, in1=abs_sums[:], op0=ALU.add, op1=ALU.add)

from contextlib import ExitStack

import concourse.mybir as mybir
from concourse.masks import make_identity

F32 = mybir.dt.float32
BF16 = mybir.dt.bfloat16
I32 = mybir.dt.int32
U32 = mybir.dt.uint32
U8 = mybir.dt.uint8
FP8 = mybir.dt.float8_e4m3fn
FP8X4 = mybir.dt.float8_e4m3fn_x4
FP4X4 = mybir.dt.float4_e2m1fn_x4
ALU = mybir.AluOpType
ACT = mybir.ActivationFunctionType
AX = mybir.AxisListType

B, K, L = 8192, 512, 256
P = 128
NT = B // P
UNIT_SIZES = [2] * 4 + [4] * 12 + [2] * 4
UNITS = [(sum(UNIT_SIZES[:i]), n) for i, n in enumerate(UNIT_SIZES)]
NU = len(UNITS)
FLOPS = 2 * 2 * B * K * K

VOLT_CHUNKS = [2, 2, 4, 8, 8, 8, 8, 8, 8, 8]
HALF = NT // 2
PIECE = 8
CAST_UNITS = (0, 1, 2)
CAST_ON_SCALAR = (1, 2)
D_ON_VECTOR = ()
ABS_ON_VECTOR = (0, 2, 3, 5, 6, 7, 9, 10, 11, 14, 18, 19)

AHEAD_UNITS = tuple(range(1, 3))

ORDER = (
    ("Z", None),
    ("W", 0),
    ("M20", 5),
    ("D0", 3),
    ("T0", 1),
    ("T1", 1),
    ("B0", 10),
    ("S", None),
    ("D1", 3),
    ("D2", 3),
    ("F0", 5),
    ("M21", 5),
    ("F1", 5),
    ("E0", 1),
    ("G", 6),
    ("E1", 1),
    ("B2", 10),
    ("D3", 3),
    ("R", 3),
    ("Q", 1),
    ("A", None),
    ("B1", 10),
    ("B3", 10),
    ("F2", 5),
    ("Y", 7),
    ("M10", 2),
    ("M11", 2),
    ("F3", 5),
)
LAG = {name: lag for name, lag in ORDER}
A_STEPS = {4 + 1 * k: k for k in range(0, 8)}
S_STEPS = {
    **{8 + s: [(0, i) for i in range(4 * s, min(4 * s + 4, 32))] for s in range(8)},
    **{17 + s: [(1, i) for i in range(2 * s, min(2 * s + 2, 16))] for s in range(8)},
}
Z_STEPS = {16: 0, 25: 1}


def tile_pinnlayer_pa_t_w4_kernel(tc, Volt_bytes, Volt_scale, IM_words, IM_scales, Ybr_words, Ybr_scales, n_o_mu_i_u, out):
    nc = tc.nc
    with ExitStack() as ctx:
        keep = ctx.enter_context(tc.tile_pool(name="keep", bufs=1))
        flow = ctx.enter_context(tc.tile_pool(name="flow", bufs=4))
        xt_pool = ctx.enter_context(tc.psum_pool(name="xt_pool", bufs=2))
        dv_pool = ctx.enter_context(tc.psum_pool(name="dv_pool", bufs=3))
        ib_pool = ctx.enter_context(tc.psum_pool(name="ib_pool", bufs=2))
        acc_pool = ctx.enter_context(tc.psum_pool(name="acc_pool", bufs=1))

        volt_view = Volt_bytes.rearrange("(p j) k -> p j k", p=P)
        mu_view = n_o_mu_i_u.rearrange("(p j) l -> p j l", p=P)

        im_scales_raw = keep.tile([P, 512], U8, align_bytes=64)
        yb_scales = keep.tile([P, 512], U8, align_bytes=64)
        nc.vector.memset(im_scales_raw[:].bitcast(I32), 0)
        nc.vector.memset(yb_scales[:].bitcast(I32), 0)
        ident_f32 = keep.tile([P, P], F32)
        make_identity(nc, ident_f32[:])
        ident_bf16 = keep.tile([P, P], BF16)
        make_identity(nc, ident_bf16[:])

        raw_of_tile = {}
        chunks = []
        j0 = 0
        for i, n in enumerate(VOLT_CHUNKS):
            volt_raw = keep.tile([P, n, K], U8, name="volt_raw_%d" % i)
            chunks.append((volt_raw, j0, n))
            for j in range(n):
                raw_of_tile[j0 + j] = (volt_raw, j)
            j0 += n

        def load_volt(i):
            t, first, n = chunks[i]
            nc.sync.dma_start(out=t[:], in_=volt_view[:, first : first + n, :])

        mu = []
        for h in range(2):
            mu_h = keep.tile([P, HALF, L], BF16, name="mu_%d" % h)
            mu.append(mu_h)

        def load_mu(k):
            h, i = divmod(PIECE * k, HALF)
            nc.sync.dma_start(out=mu[h][:, i : i + PIECE, :], in_=mu_view[:, PIECE * k : PIECE * (k + 1), :])

        load_volt(0)
        scale_cols = keep.tile([P, 4], F32)
        nc.sync.dma_start(out=scale_cols[:], in_=Volt_scale.rearrange("o (p t) -> p (o t)", t=4))
        im_words_raw = keep.tile([P, 1024], U8)
        nc.sync.dma_start(out=im_words_raw[:], in_=IM_words[0])
        for q in range(4):
            nc.sync.dma_start(out=im_scales_raw[32 * q : 32 * q + 4, :].bitcast(I32), in_=IM_scales[0, 4 * q : 4 * q + 4, :].bitcast(I32))
        load_volt(1)
        load_volt(2)
        scale_rows = keep.tile([P, 4, K], F32)
        nc.sync.dma_start(out=scale_rows[:, 0, :], in_=Volt_scale.rearrange("o k -> (o k)").partition_broadcast(P))
        yb_words = keep.tile([P, 1024], U8, align_bytes=64)
        nc.sync.dma_start(out=yb_words[:], in_=Ybr_words[0])
        for q in range(4):
            nc.sync.dma_start(out=yb_scales[32 * q : 32 * q + 4, :].bitcast(I32), in_=Ybr_scales[0, 4 * q : 4 * q + 4, :].bitcast(I32))
        load_mu(0)
        load_volt(3)
        load_mu(1)
        load_volt(4)
        load_volt(5)
        load_mu(2)
        load_volt(6)
        load_mu(3)
        load_volt(7)
        load_mu(4)
        load_volt(8)
        load_mu(5)
        load_volt(9)
        load_mu(6)
        load_mu(7)

        mag_0 = keep.tile([P, HALF, L], BF16)
        neg_1 = keep.tile([P, HALF, L], BF16)
        mag = (mag_0, mu[1])
        plus_half = keep.tile([P, P], BF16)
        minus_half = keep.tile([P, P], BF16)
        nc.vector.tensor_scalar(out=plus_half[:], in0=ident_bf16[:], scalar1=0.5, scalar2=None, op0=ALU.mult)
        nc.vector.tensor_scalar(out=minus_half[:], in0=ident_bf16[:], scalar1=-0.5, scalar2=None, op0=ALU.mult)
        sq_sums = keep.tile([P, NT], F32)
        abs_sums = keep.tile([P, NT], F32)
        neg_sums = keep.tile([P, NT], F32)
        final = keep.tile([P, NT], F32)

        rows_of, xt_of, plain_of, quant_of, dv_of, ib_of, sq_of, cur_of, acc_of = ({} for i in range(9))

        def stage_w(u):
            c0, n = UNITS[u]
            rows = flow.tile([P, n * K], BF16, tag="rows", name="rows")
            rows_of[u] = rows
            t, j = raw_of_tile[c0]
            src = t[:, j : j + n, :].rearrange("p j k -> p (j k)").bitcast(FP8)
            if u in CAST_UNITS:
                if u in CAST_ON_SCALAR:
                    nc.scalar.copy(out=rows[:], in_=src)
                else:
                    nc.vector.tensor_copy(out=rows[:], in_=src)
            else:
                nc.vector.tensor_tensor(out=rows[:], in0=src, in1=scale_rows[:, 0:n, :].rearrange("p j k -> p (j k)"), op=ALU.mult)

        def stage_t(u, g):
            c0, n = UNITS[u]
            words = rows_of[u][:].bitcast(F32)
            if 2 * g < n:
                xt = xt_pool.tile([P, 2, 2 * P], F32, tag="xt", name="xt")
                xt_of[c0 + 2 * g] = xt
                for i in range(2):
                    j = 2 * g + i
                    for h in range(2):
                        nc.tensor.transpose(xt[:, h, P * i : P * (i + 1)], words[:, 256 * j + h : 256 * (j + 1) : 2], ident_f32[:])

        def stage_e(u, g):
            c0, n = UNITS[u]
            if 2 * g < n:
                xt = xt_of[c0 + 2 * g]
                dst = plain_tile(u + LAG["Q"])[:, 2 * K * g : 2 * K * (g + 1)]
                if u in CAST_UNITS:
                    nc.vector.tensor_tensor(
                        out=dst.rearrange("p (c h e) -> p c h e", h=2, e=2),
                        in0=xt[:].bitcast(BF16).rearrange("p h (c e) -> p c h e", e=2),
                        in1=scale_cols[:].rearrange("p (h e) -> p h e", e=2).unsqueeze(1).to_broadcast([P, 2 * P, 2, 2]),
                        op=ALU.mult,
                    )
                else:
                    nc.scalar.copy(out=dst.bitcast(F32).rearrange("p (c h) -> p c h", h=2), in_=xt[:].rearrange("p h c -> p c h"))

        def widths(step):
            u, v = step - LAG["Q"], step - LAG["R"]
            return (UNITS[u][1] if 0 <= u < NU else 0), (UNITS[v][1] if 0 <= v < NU else 0)

        def plain_tile(step):
            if step not in plain_of:
                m, n = widths(step)
                plain = flow.tile([P, (m + n) * K], BF16, tag="plain", name="plain", bufs=3, align_bytes=64)
                plain_of[step] = plain
                codes = flow.tile([P, (m + n) * P], U32, tag="codes", name="codes", bufs=3, align_bytes=64)
                scales = flow.tile([P, (m + n) * P], U8, tag="scales", name="scales", bufs=3, align_bytes=64)
                quant_of[step] = (codes, scales)
            return plain_of[step]

        def quantise(step, first, last):
            codes, scales = quant_of[step]
            nc.vector.quantize_mx(
                out=codes[:, P * first : P * last].bitcast(FP8X4),
                scales=scales[:, P * first : P * last],
                in_=plain_of[step][:, K * first : K * last],
            )

        def stage_q(u):
            m, n = widths(u + LAG["Q"])
            quantise(u + LAG["Q"], 0, m + n if m + n in (2, 4, 8) else m)

        def stage_r(u):
            m, n = widths(u + LAG["R"])
            if m == 0 or m + n not in (2, 4, 8):
                quantise(u + LAG["R"], m, m + n)

        def stage_m1(u, g):
            c0, n = UNITS[u]
            xq, xs = quant_of[u + LAG["Q"]]
            for j in range(2 * g, min(2 * g + 2, n)):
                dv = dv_pool.tile([P, 4, P], F32, tag="dv", name="dv")
                dv_of[c0 + j] = dv
                for t in range(4):
                    nc.tensor.matmul_mx(
                        out=dv[:, t, :],
                        lhsT=im_words[:, 256 * t : 256 * (t + 1)].bitcast(FP4X4),
                        lhsT_scale=im_scales[:, P * t : P * (t + 1)],
                        rhs=xq[:, P * j : P * (j + 1)].bitcast(FP8X4),
                        rhs_scale=xs[:, P * j : P * (j + 1)],
                        start=True,
                        stop=True,
                    )

        def stage_d(u, half):
            c0, n = UNITS[u]
            m, n = widths(u + LAG["R"])
            for j in range(half, min(half + 1, n)):
                dst = plain_tile(u + LAG["R"])[:, K * (m + j) : K * (m + j + 1)].rearrange("p (c t) -> p c t", t=4)
                src = dv_of[c0 + j][:].rearrange("p t c -> p c t")
                if c0 + j in D_ON_VECTOR:
                    nc.vector.tensor_copy(out=dst, in_=src)
                else:
                    nc.scalar.copy(out=dst, in_=src)

        def stage_m2(u, g):
            c0, n = UNITS[u]
            codes, scales = quant_of[u + LAG["R"]]
            m, n = widths(u + LAG["R"])
            dvq, dvs = codes[:, P * m : P * (m + n)], scales[:, P * m : P * (m + n)]
            for j in range(2 * g, min(2 * g + 2, n)):
                ib = ib_pool.tile([P, 512], F32, tag="ib", name="ib")
                ib_of[c0 + j] = ib
                nc.tensor.matmul_mx(
                    out=ib[:],
                    lhsT=dvq[:, P * j : P * (j + 1)].bitcast(FP8X4),
                    lhsT_scale=dvs[:, P * j : P * (j + 1)],
                    rhs=yb_words[:].bitcast(FP4X4),
                    rhs_scale=yb_scales[:],
                    start=True,
                    stop=True,
                )

        def stage_f(u, half):
            c0, n = UNITS[u]
            if half == 0:
                sq = flow.tile([P, n, 512], F32, tag="sq", name="sq", bufs=3)
                sq_of[u] = sq
            sq = sq_of[u]
            for j in range(half, min(half + 1, n)):
                c = c0 + j
                nc.scalar.activation(out=sq[:, j, :], in_=ib_of[c][:], func=ACT.Square, accum_out=sq_sums[:, c : c + 1])

        def stage_a(step):
            if step in A_STEPS:
                h, i = divmod(PIECE * A_STEPS[step], HALF)
                sel = slice(i, i + PIECE)
                src = mu[h][:, sel, :].rearrange("p j l -> p (j l)")
                if h == 1:
                    nc.vector.tensor_scalar(
                        out=neg_1[:, sel, :].rearrange("p j l -> p (j l)"), in0=src, scalar1=-1.0, scalar2=0.0, op0=ALU.mult, op1=ALU.max
                    )
                nc.vector.tensor_scalar(
                    out=mag[h][:, sel, :].rearrange("p j l -> p (j l)").bitcast(I32),
                    in0=src.bitcast(I32),
                    scalar1=0x7FFF7FFF,
                    scalar2=None,
                    op0=ALU.bitwise_and,
                )

        def stage_g(u):
            c0, n = UNITS[u]
            cur = flow.tile([P, n, L], F32, tag="cur", name="cur", bufs=6)
            cur_of[u] = cur
            sq = sq_of[u]
            nc.vector.scalar_tensor_tensor(out=cur[:], in0=sq[:, :, 0:L], scalar=-1.0, in1=sq[:, :, L : 2 * L], op0=ALU.add, op1=ALU.add)

        def stage_y(u):
            c0, n = UNITS[u]
            cur = cur_of[u]
            h, i = divmod(c0, HALF)
            nc.vector.scalar_tensor_tensor(out=cur[:], in0=mag[h][:, i : i + n, :], scalar=0.5, in1=cur[:], op0=ALU.add, op1=ALU.mult)

        def stage_b(u, j):
            c0, n = UNITS[u]
            if u in ABS_ON_VECTOR:
                if j == 0:
                    nc.vector.tensor_reduce(out=abs_sums[:, c0 : c0 + n], in_=cur_of[u][:], axis=AX.X, op=ALU.add, apply_absolute_value=True)
            elif j < n:
                junk = flow.tile([P, L], F32, tag="junk", name="junk", bufs=2)
                nc.scalar.activation(out=junk[:], in_=cur_of[u][:, j, :], func=ACT.Abs, accum_out=abs_sums[:, c0 + j : c0 + j + 1])

        def stage_s(step):
            for h, i in S_STEPS.get(step, ()):
                last = 31 if h == 0 else 15
                if i == 0:
                    acc = acc_pool.tile([P, 512], F32, tag="acc", name="acc")
                    acc_of[h] = acc
                if h == 1:
                    weights, values = ident_bf16, neg_1
                elif i < 16:
                    weights, values = plus_half, mag[0]
                else:
                    weights, values = minus_half, mu[0]
                c = i % 16
                nc.tensor.matmul(acc_of[h][:], lhsT=weights[:], rhs=values[:, :, 16 * c : 16 * (c + 1)], start=(i == 0), stop=(i == last))

        def stage_z(step):
            if step in Z_STEPS:
                h = Z_STEPS[step]
                nc.vector.tensor_reduce(
                    out=neg_sums[:, HALF * h : HALF * (h + 1)],
                    in_=acc_of[h][:].rearrange("p (j l) -> p j l", l=16),
                    axis=AX.X,
                    op=ALU.add,
                )

        stages = {"W": stage_w, "Q": stage_q, "R": stage_r, "A": stage_a, "G": stage_g, "Y": stage_y, "S": stage_s, "Z": stage_z}
        for g in range(2):
            stages["T%d" % g] = lambda u, g=g: stage_t(u, g)
            stages["E%d" % g] = lambda u, g=g: stage_e(u, g)
            stages["M1%d" % g] = lambda u, g=g: stage_m1(u, g)
            stages["M2%d" % g] = lambda u, g=g: stage_m2(u, g)
        for j in range(4):
            stages["D%d" % j] = lambda u, j=j: stage_d(u, j)
            stages["F%d" % j] = lambda u, j=j: stage_f(u, j)
            stages["B%d" % j] = lambda u, j=j: stage_b(u, j)
        deepest = max(lag for name, lag in ORDER if lag is not None)
        im_words = keep.tile([P, 1024], U8, align_bytes=64)
        im_scales = keep.tile([P, 512], U8, align_bytes=64)

        def permute_im():
            nc.vector.tensor_copy(
                out=im_words[:].rearrange("p (t m e) -> p m t e", t=4, e=2),
                in_=im_words_raw[:].rearrange("p (m t e) -> p m t e", t=4, e=2),
            )
            nc.vector.tensor_copy(
                out=im_scales[:].rearrange("p (t m) -> p m t", t=4),
                in_=im_scales_raw[:].rearrange("p (m t) -> p m t", t=4),
            )

        with tc.manual_schedule(engines={mybir.EngineType.PE, mybir.EngineType.Activation, mybir.EngineType.DVE}):
            for step in range(NU + deepest):
                for name, lag in ORDER:
                    if lag is None:
                        stages[name](step)
                    elif 0 <= step - lag < NU and not (name == "W" and step in AHEAD_UNITS):
                        stages[name](step - lag)
                    if name == "W":
                        if step == 1:
                            permute_im()
                        if step == 0:
                            for u in AHEAD_UNITS:
                                stage_w(u)
                        if step == 2:
                            nc.scalar.copy(out=scale_rows[:, 1, :], in_=scale_rows[:, 0, :])
                        if step == 3:
                            nc.scalar.copy(out=scale_rows[:, 2:4, :], in_=scale_rows[:, 0:2, :])

        nc.vector.scalar_tensor_tensor(out=final[:], in0=sq_sums[:], scalar=0.5, in1=neg_sums[:], op0=ALU.mult, op1=ALU.add)
        nc.vector.scalar_tensor_tensor(out=final[:], in0=final[:], scalar=-0.5 * L, in1=abs_sums[:], op0=ALU.add, op1=ALU.add)
        nc.sync.dma_start(out=out.rearrange("(p j) -> p j", p=P), in_=final[:])
